import numpy as np
import ml_dtypes


def mxq(x, axis, fmt="e4m3"):
    dtype, down = {"e4m3": (ml_dtypes.float8_e4m3fn, 7), "e5m2": (ml_dtypes.float8_e5m2, 14)}[fmt]
    v = np.moveaxis(np.asarray(x, np.float32).astype(ml_dtypes.bfloat16).astype(np.float64), axis, -1)
    blocks = v.reshape(v.shape[:-1] + (-1, 32))
    amax = np.abs(blocks).max(-1, keepdims=True)
    byte = np.maximum(np.where(amax > 0, np.frexp(amax)[1] - 1 + 127, 0) - down, 1)
    scale = np.exp2(byte - 127.0)
    codes = (blocks / scale).astype(np.float32).astype(dtype).astype(np.float64)
    return np.moveaxis((codes * scale).reshape(v.shape), -1, axis)


WIDE = False


def mx_kscale(k):
    if not WIDE:
        return np.ones(k)
    levels = np.array([10, -10, 5, -5, 0])
    if k % 512:
        return np.exp2(np.random.permutation(np.resize(levels, k // 32))).repeat(32)
    a = np.empty((k // 512, 16))
    for p in range(k // 512):
        a[p, :8] = np.random.permutation(np.resize(levels, 8))
        for g in range(8):
            far = levels[np.abs(levels - a[p, g]) >= 10]
            a[p, g + 8] = far[np.random.randint(len(far))]
    return np.exp2(a.ravel()).repeat(32)


BF16 = ml_dtypes.bfloat16


def bf(x):
    return np.asarray(x, np.float32).astype(BF16)


def f64(x):
    return np.asarray(x).astype(np.float64)


E2M1 = np.array([0.0, 0.5, 1.0, 1.5, 2.0, 3.0, 4.0, 6.0, -0.0, -0.5, -1.0, -1.5, -2.0, -3.0, -4.0, -6.0])


def pack_weight(w, fmt):
    k, n = w.shape
    w = f64(bf(w)).reshape(k // 32, 32, n)
    amax = np.abs(w).max(1)
    if fmt == "e4m3":
        byte = np.frexp(amax)[1] - 1 + 127 - 7
    else:
        mant, ex = np.frexp(amax / 6.0)
        byte = np.where(mant > 0.5, ex, ex - 1) + 127
    byte = np.clip(np.where(amax > 0, byte, 1), 1, 254)
    scaled = (w * np.exp2(127.0 - byte)[:, None, :]).reshape(k, n).astype(np.float32)
    by_word = np.ascontiguousarray(scaled.reshape(k // 512, 128, 4, n).transpose(0, 1, 3, 2))
    if fmt == "e4m3":
        words = by_word.astype(ml_dtypes.float8_e4m3fn).view(np.uint8)
    else:
        c = by_word.astype(ml_dtypes.float4_e2m1fn).view(np.uint8) & 0xF
        words = c[..., 0::2] | (c[..., 1::2] << 4)
    return np.ascontiguousarray(words), np.ascontiguousarray(byte.astype(np.uint8).reshape(k // 512, 16, n))


def unpack_weight(words, scales, fmt):
    g, p, n, _ = words.shape
    if fmt == "e4m3":
        vals = np.ascontiguousarray(words).view(ml_dtypes.float8_e4m3fn).astype(np.float64)
    else:
        nib = np.empty((g, p, n, 4), np.uint8)
        nib[..., 0::2] = words & 0xF
        nib[..., 1::2] = words >> 4
        vals = E2M1[nib]
    vals = vals * np.repeat(np.exp2(scales.astype(np.float64) - 127.0), 8, axis=1)[..., None]
    return vals.transpose(0, 1, 3, 2).reshape(g * 512, n)
def pack4(w):
    words, scales = pack_weight(w, "e2m1")
    return words.reshape(words.shape[0], 128, -1), scales


def unpack4(words, scales):
    return unpack_weight(words.reshape(words.shape[0], 128, -1, 2), scales, "e2m1")


B, IN, HID, BLK, OUT = 4096, 512, 1024, 512, 10
NB = HID // BLK


def draw0():
    s = mx_kscale(IN)
    t = np.tile(mx_kscale(BLK), NB)
    x = bf(np.random.standard_normal((B, IN)) * s)
    W1 = np.random.standard_normal((HID, IN)) / np.sqrt(IN) / s * t[:, None]
    W1_words, W1_scales = pack4(W1.T)
    return {
        "x": x,
        "W1_words": W1_words,
        "W1_scales": W1_scales,
        "b1": bf(np.random.standard_normal(HID) * 0.3 * t),
        "Wb": bf(np.random.standard_normal((NB, BLK, BLK)) * 1.4 / np.sqrt(BLK) / t.reshape(NB, 1, BLK)),
        "bb": bf(np.random.standard_normal(HID) * 0.3),
    }


def core(x, W1_words, W1_scales, b1, Wb, bb):
    h = np.maximum((mxq(f64(x), 1, "e4m3") @ unpack4(W1_words, W1_scales)) + f64(b1), 0.0)
    hb = h.reshape(B, NB, BLK)
    yb = (mxq(hb, 2, "e4m3").transpose(1, 0, 2) @ mxq(f64(Wb), 2, "e4m3").transpose(0, 2, 1)).transpose(1, 0, 2)
    return np.maximum(yb.reshape(B, HID) + f64(bb), 0.0)


def e4m3fn_bytes(y):
    return np.clip(np.asarray(y, np.float64), -448.0, 448.0).astype(np.float32).astype(ml_dtypes.float8_e4m3fn).view(np.uint8)


def e4m3fn_values(b):
    return np.asarray(b, np.uint8).view(ml_dtypes.float8_e4m3fn).astype(np.float64)


def setup_inputs():
    d = draw0()
    x0 = np.asarray(d['x']).astype(np.float64)
    s = (np.max(np.abs(x0), axis=(0,), keepdims=True) / 448.0).astype(np.float32)
    out = {}
    for k, v in d.items():
        if k == 'x':
            out['x_bytes'] = e4m3fn_bytes(x0 / s.astype(np.float64))
            out['x_scale'] = s
        else:
            out[k] = v
    return out


def reference(x_bytes, x_scale, W1_words, W1_scales, b1, Wb, bb):
    return core(e4m3fn_values(x_bytes) * x_scale.astype(np.float64), W1_words, W1_scales, b1, Wb, bb)

@@ -1,0 +1,292 @@
+from contextlib import ExitStack
+
+import concourse.mybir as mybir
+from concourse.masks import make_identity
+
+B, IN, HID, BLK = 4096, 512, 1024, 512
+FLOPS = 2 * B * IN * HID + 2 * B * HID * BLK
+
+F32 = mybir.dt.float32
+BF16 = mybir.dt.bfloat16
+U32 = mybir.dt.uint32
+I32 = mybir.dt.int32
+U8 = mybir.dt.uint8
+FP8 = mybir.dt.float8_e4m3fn
+FP8X4 = mybir.dt.float8_e4m3fn_x4
+FP4X4 = mybir.dt.float4_e2m1fn_x4
+ALU = mybir.AluOpType
+ACT = mybir.ActivationFunctionType
+
+P = 128
+GROUPS = [2, 4, 4, 4, 4, 4, 4, 4, 2]
+FLT_MAX = 3.4028234663852886e38
+
+
+def tile_blockdiagmnistconvertible_pa_t_w4_kernel(tc, x_bytes, x_scale, W1_words, W1_scales, b1, Wb, bb, out):
+    nc = tc.nc
+    L = len(GROUPS)
+    first = [P * sum(GROUPS[:g]) for g in range(L)]
+
+    with ExitStack() as ctx:
+        keep = ctx.enter_context(tc.tile_pool(name="keep", bufs=1))
+        work = ctx.enter_context(tc.tile_pool(name="work", bufs=3))
+        psum = ctx.enter_context(tc.psum_pool(name="psum", bufs=2))
+
+        ident = keep.tile([P, P], F32, name="ident")
+        sc = keep.tile([P, IN], F32, name="sc")
+        w1r = keep.tile([P, 2048], U8, name="w1r")
+        w1p = keep.tile([P, 2, 4, P, 2], U8, name="w1p", align_bytes=64)
+        wsr = keep.tile([P, HID], U8, name="wsr", align_bytes=64)
+        wsp = keep.tile([P, 2, 4, P], U8, name="wsp", align_bytes=64)
+        b1c = keep.tile([P, 2, 4], BF16, name="b1c")
+        bbc = keep.tile([P, 4], BF16, name="bbc")
+        bbr = keep.tile([P, BLK], BF16, name="bbr")
+        warm = keep.tile([P, 1], F32, name="warm")
+        xb = [keep.tile([P, GROUPS[g], IN], U8, name=f"xb{g}") for g in range(L)]
+        wbr = [keep.tile([P, 4, BLK], BF16, name=f"wbr{n}") for n in range(2)]
+        wbc = [keep.tile([P, BLK], U32, name=f"wbc{n}", align_bytes=64) for n in range(2)]
+        wbs = [keep.tile([P, BLK], U8, name=f"wbs{n}", align_bytes=64) for n in range(2)]
+
+        def load_x(g):
+            src = x_bytes[first[g] : first[g] + P * GROUPS[g], :].rearrange("(p a) k -> p a k", a=GROUPS[g])
+            nc.sync.dma_start(out=xb[g][:], in_=src)
+
+        nc.vector.memset(warm[:], 0.0)
+        nc.vector.memset(wsr[:].bitcast(I32), 0)
+        nc.scalar.activation(out=warm[:], in_=warm[:], func=ACT.Relu)
+        make_identity(nc, ident[:])
+        load_x(0)
+        nc.sync.dma_start(out=sc[:], in_=x_scale.rearrange("o k -> (o k)").partition_broadcast(P))
+        nc.sync.dma_start(out=w1r[:], in_=W1_words[0])
+        for q in range(4):
+            nc.sync.dma_start(
+                out=wsr[32 * q : 32 * q + 4, :].bitcast(I32), in_=W1_scales[0, 4 * q : 4 * q + 4, :].bitcast(I32)
+            )
+        load_x(1)
+        nc.sync.dma_start(out=b1c[:], in_=b1.rearrange("(n p t) -> p n t", n=2, t=4))
+        nc.sync.dma_start(out=wbr[1][:], in_=Wb[1].rearrange("(p t) k -> p t k", t=4))
+        nc.sync.dma_start(out=bbc[:], in_=bb[BLK:HID].rearrange("(p t) -> p t", t=4))
+        nc.sync.dma_start(out=wbr[0][:], in_=Wb[0].rearrange("(t p) k -> p t k", p=P))
+        nc.sync.dma_start(out=bbr[:], in_=bb[0:BLK].partition_broadcast(P))
+        for g in range(2, L):
+            load_x(g)
+
+        xs, xg, xc, xsc = {}, {}, {}, {}
+        xt, hp, hg, hc, hs = {}, {}, {}, {}, {}
+        y1, y0, yt, tr, o = {}, {}, {}, {}, {}
+
+        def width(g):
+            return P * GROUPS[g]
+
+        def halves(g):
+            return GROUPS[g] // 2
+
+        def scale_x(g, h):
+            if h == 0:
+                xs[g] = work.tile([P, GROUPS[g], IN], BF16, name="xs", tag="xs")
+            if h >= halves(g):
+                return
+            for a in (2 * h, 2 * h + 1):
+                nc.vector.tensor_tensor(out=xs[g][:, a, :], in0=xb[g][:, a, :].bitcast(FP8), in1=sc[:], op=ALU.mult)
+
+        def turn(rows, a0, key):
+            xt[key] = psum.tile([P, 2, 2 * P], F32, name="xt", tag="xt", bufs=2)
+            for a in (0, 1):
+                words = rows[:, a0 + a, :].bitcast(F32)
+                for u in (0, 1):
+                    nc.tensor.transpose(xt[key][:, u, a * P : (a + 1) * P], words[:, u : 2 * P : 2], ident[:])
+
+        def turn_x(g, h):
+            if h < halves(g):
+                turn(xs[g], 2 * h, (g, h))
+
+        def unload(dst, h, key):
+            cols = dst[:, 2 * P * h : 2 * P * (h + 1), :].rearrange("p r t -> p (r t)").bitcast(F32)
+            nc.scalar.copy(out=cols.rearrange("p (r u) -> p r u", u=2), in_=xt[key][:].rearrange("p u r -> p r u"))
+
+        def unload_x(g, h):
+            if h == 0:
+                xg[g] = work.tile([P, width(g), 4], BF16, name="xg", tag="xg", align_bytes=64)
+            if h < halves(g):
+                unload(xg[g], h, (g, h))
+
+        def quantize(src, codes, scales):
+            nc.vector.quantize_mx(out=codes.bitcast(FP8X4), scales=scales, in_=src.rearrange("p r t -> p (r t)"))
+
+        def quant_x(g):
+            xc[g] = work.tile([P, width(g)], U32, name="xc", tag="xc", align_bytes=64)
+            xsc[g] = work.tile([P, width(g)], U8, name="xsc", tag="xsc", align_bytes=64)
+            quantize(xg[g][:], xc[g][:], xsc[g][:])
+
+        def stage1(g, n, t):
+            acc = psum.tile([P, width(g)], F32, name="h", tag="h", bufs=2)
+            nc.tensor.matmul_mx(
+                out=acc[:],
+                lhsT=w1p[:, n, t].rearrange("p m b -> p (m b)").bitcast(FP4X4),
+                lhsT_scale=wsp[:, n, t, :],
+                rhs=xc[g][:].bitcast(FP8X4),
+                rhs_scale=xsc[g][:],
+                start=True,
+                stop=True,
+            )
+            if t == 0:
+                hp[g, n] = work.tile([P, 4, width(g)], BF16, name="hp", tag="hp", bufs=4)
+            nc.scalar.activation(out=hp[g, n][:, t, :], in_=acc[:], func=ACT.Relu, bias=b1c[:, n, t : t + 1])
+
+        def interleave(g, n):
+            hg[g, n] = work.tile([P, width(g), 4], BF16, name="hg", tag="hg", align_bytes=64)
+            nc.vector.tensor_copy(
+                out=hg[g, n][:].rearrange("p (c i) t -> p c t i", i=4),
+                in_=hp[g, n][:].rearrange("p t (c i) -> p c t i", i=4),
+            )
+
+        def quant_h(g, n):
+            hc[g, n] = work.tile([P, width(g)], U32, name="hc", tag="hc", align_bytes=64, bufs=4)
+            hs[g, n] = work.tile([P, width(g)], U8, name="hs", tag="hs", align_bytes=64, bufs=4)
+            quantize(hg[g, n][:], hc[g, n][:], hs[g, n][:])
+
+        def stage2_channels(g, t):
+            y1[g, t] = psum.tile([P, width(g)], F32, name="y", tag="y", bufs=2)
+            cols = slice(t * P, (t + 1) * P)
+            nc.tensor.matmul_mx(
+                out=y1[g, t][:],
+                lhsT=wbc[1][:, cols].bitcast(FP8X4),
+                lhsT_scale=wbs[1][:, cols],
+                rhs=hc[g, 1][:].bitcast(FP8X4),
+                rhs_scale=hs[g, 1][:],
+                start=True,
+                stop=True,
+            )
+
+        def relu_channels(g, t):
+            yt[g, t] = work.tile([P, width(g)], F32, name="yt", tag="yt", bufs=8)
+            nc.scalar.activation(out=yt[g, t][:], in_=y1[g, t][:], func=ACT.Relu, bias=bbc[:, t : t + 1])
+
+        def turn_back(g, a):
+            if a >= GROUPS[g]:
+                return
+            tr[g, a] = psum.tile([P, 4, P], F32, name="tr", tag="tr", bufs=2)
+            for t in range(4):
+                nc.tensor.transpose(tr[g, a][:, t, :], yt[g, t][:, a * P : (a + 1) * P], ident[:])
+
+        def store_turned(g, a, on_vector):
+            if a >= GROUPS[g]:
+                return
+            dst = o[g][:, a, BLK:HID].rearrange("p (r t) -> p r t", t=4)
+            src = tr[g, a][:].rearrange("p t r -> p r t")
+            if on_vector:
+                nc.vector.tensor_copy(out=dst, in_=src)
+            else:
+                nc.scalar.copy(out=dst, in_=src)
+            rows = out[first[g] : first[g] + width(g), :].rearrange("(p a) c -> p a c", a=GROUPS[g])
+            nc.sync.dma_start(out=rows[:, a, :], in_=o[g][:, a, :])
+
+        def stage2_tokens(g, a):
+            if a >= GROUPS[g]:
+                return
+            y0[g, a] = psum.tile([P, BLK], F32, name="y", tag="y", bufs=2)
+            cols = slice(a * P, (a + 1) * P)
+            nc.tensor.matmul_mx(
+                out=y0[g, a][:],
+                lhsT=hc[g, 0][:, cols].bitcast(FP8X4),
+                lhsT_scale=hs[g, 0][:, cols],
+                rhs=wbc[0][:].bitcast(FP8X4),
+                rhs_scale=wbs[0][:],
+                start=True,
+                stop=True,
+            )
+
+        def bias_tokens(g, a):
+            if a >= GROUPS[g]:
+                return
+            if a == 0:
+                o[g] = work.tile([P, GROUPS[g], HID], F32, name="o", tag="o")
+            part = o[g][:, a, 0:BLK]
+            nc.vector.tensor_tensor(out=part, in0=y0[g, a][:], in1=bbr[:], op=ALU.add)
+            nc.gpsimd.tensor_scalar(out=part, in0=part, scalar1=FLT_MAX, scalar2=0.0, op0=ALU.min, op1=ALU.max)
+
+        def weights2(n):
+            wg = work.tile([P, BLK, 4], BF16, name="wg", tag="wg", align_bytes=64, bufs=2)
+            for h in (0, 1):
+                turn(wbr[n], 2 * h, ("w", n, h))
+                unload(wg, h, ("w", n, h))
+            quantize(wg[:], wbc[n][:], wbs[n][:])
+
+        def permute_w1(n):
+            nc.vector.tensor_copy(
+                out=w1p[:, n], in_=w1r[:].rearrange("p (n m t b) -> p n t m b", n=2, t=4, b=2)[:, n]
+            )
+            nc.gpsimd.tensor_copy(out=wsp[:, n], in_=wsr[:].rearrange("p (n m t) -> p n t m", n=2, t=4)[:, n])
+
+        def slot(g):
+            now, prev, nxt, far = 0 <= g < L, 0 <= g - 1 < L, 0 <= g + 1 < L, 0 <= g + 2 < L
+            if prev:
+                bias_tokens(g - 1, 0)
+            if now:
+                stage1(g, 1, 0)
+                stage1(g, 1, 1)
+            if prev:
+                stage2_tokens(g - 1, 2)
+                bias_tokens(g - 1, 1)
+            if now:
+                stage1(g, 1, 2)
+            if prev:
+                stage2_tokens(g - 1, 3)
+            if now:
+                stage1(g, 1, 3)
+            if prev:
+                bias_tokens(g - 1, 2)
+                bias_tokens(g - 1, 3)
+                turn_back(g - 1, 0)
+                turn_back(g - 1, 1)
+            if now:
+                interleave(g, 1)
+                for t in range(4):
+                    stage1(g, 0, t)
+            if prev:
+                store_turned(g - 1, 0, False)
+                store_turned(g - 1, 1, GROUPS[g - 1] == 2)
+            if far:
+                scale_x(g + 2, 0)
+            if g == -2:
+                permute_w1(1)
+                permute_w1(0)
+            if now:
+                quant_h(g, 1)
+                stage2_channels(g, 0)
+                stage2_channels(g, 1)
+                interleave(g, 0)
+            if prev:
+                turn_back(g - 1, 2)
+                turn_back(g - 1, 3)
+                store_turned(g - 1, 2, False)
+            if nxt:
+                unload_x(g + 1, 0)
+                unload_x(g + 1, 1)
+            if g == -1:
+                quant_x(0)
+                weights2(1)
+            if g == 0:
+                weights2(0)
+            if far:
+                turn_x(g + 2, 0)
+                scale_x(g + 2, 1)
+                turn_x(g + 2, 1)
+            if now:
+                relu_channels(g, 0)
+                stage2_channels(g, 2)
+                relu_channels(g, 1)
+                stage2_channels(g, 3)
+                relu_channels(g, 2)
+                relu_channels(g, 3)
+                quant_h(g, 0)
+            if prev:
+                store_turned(g - 1, 3, True)
+            if nxt and g >= 0:
+                quant_x(g + 1)
+            if now:
+                stage2_tokens(g, 0)
+                stage2_tokens(g, 1)
+
+        for g in range(-2, L + 1):
+            slot(g)

@@ -19,7 +19,6 @@ ACT = mybir.ActivationFunctionType
 
 P = 128
 GROUPS = [2, 4, 4, 4, 4, 4, 4, 4, 2]
-FLT_MAX = 3.4028234663852886e38
 
 
 def tile_blockdiagmnistconvertible_pa_t_w4_kernel(tc, x_bytes, x_scale, W1_words, W1_scales, b1, Wb, bb, out):
@@ -203,7 +202,9 @@ def tile_blockdiagmnistconvertible_pa_t_w4_kernel(tc, x_bytes, x_scale, W1_words
                 o[g] = work.tile([P, GROUPS[g], HID], F32, name="o", tag="o")
             part = o[g][:, a, 0:BLK]
             nc.vector.tensor_tensor(out=part, in0=y0[g, a][:], in1=bbr[:], op=ALU.add)
-            nc.gpsimd.tensor_scalar(out=part, in0=part, scalar1=FLT_MAX, scalar2=0.0, op0=ALU.min, op1=ALU.max)
+            if a % 2 == 1:
+                pair = o[g][:, a - 1 : a + 1, 0:BLK]
+                nc.vector.tensor_scalar(out=pair, in0=pair, scalar1=0.0, scalar2=None, op0=ALU.max)
 
         def weights2(n):
             wg = work.tile([P, BLK, 4], BF16, name="wg", tag="wg", align_bytes=64, bufs=2)
@@ -281,7 +282,7 @@ def tile_blockdiagmnistconvertible_pa_t_w4_kernel(tc, x_bytes, x_scale, W1_words
                 relu_channels(g, 3)
                 quant_h(g, 0)
             if prev:
-                store_turned(g - 1, 3, True)
+                store_turned(g - 1, 3, False)
             if nxt and g >= 0:
                 quant_x(g + 1)
             if now:

from contextlib import ExitStack

import concourse.mybir as mybir
from concourse.masks import make_identity

B, IN, HID, BLK = 4096, 512, 1024, 512
FLOPS = 2 * B * IN * HID + 2 * B * HID * BLK

F32 = mybir.dt.float32
BF16 = mybir.dt.bfloat16
U32 = mybir.dt.uint32
I32 = mybir.dt.int32
U8 = mybir.dt.uint8
FP8 = mybir.dt.float8_e4m3fn
FP8X4 = mybir.dt.float8_e4m3fn_x4
FP4X4 = mybir.dt.float4_e2m1fn_x4
ALU = mybir.AluOpType
ACT = mybir.ActivationFunctionType

P = 128
GROUPS = [2, 4, 4, 4, 4, 4, 4, 4, 2]


def tile_blockdiagmnistconvertible_pa_t_w4_kernel(tc, x_bytes, x_scale, W1_words, W1_scales, b1, Wb, bb, out):
    nc = tc.nc
    L = len(GROUPS)
    first = [P * sum(GROUPS[:g]) for g in range(L)]

    with ExitStack() as ctx:
        keep = ctx.enter_context(tc.tile_pool(name="keep", bufs=1))
        work = ctx.enter_context(tc.tile_pool(name="work", bufs=3))
        psum = ctx.enter_context(tc.psum_pool(name="psum", bufs=2))

        ident = keep.tile([P, P], F32, name="ident")
        sc = keep.tile([P, IN], F32, name="sc")
        w1r = keep.tile([P, 2048], U8, name="w1r")
        w1p = keep.tile([P, 2, 4, P, 2], U8, name="w1p", align_bytes=64)
        wsr = keep.tile([P, HID], U8, name="wsr", align_bytes=64)
        wsp = keep.tile([P, 2, 4, P], U8, name="wsp", align_bytes=64)
        b1c = keep.tile([P, 2, 4], BF16, name="b1c")
        bbc = keep.tile([P, 4], BF16, name="bbc")
        bbr = keep.tile([P, BLK], BF16, name="bbr")
        warm = keep.tile([P, 1], F32, name="warm")
        xb = [keep.tile([P, GROUPS[g], IN], U8, name=f"xb{g}") for g in range(L)]
        wbr = [keep.tile([P, 4, BLK], BF16, name=f"wbr{n}") for n in range(2)]
        wbc = [keep.tile([P, BLK], U32, name=f"wbc{n}", align_bytes=64) for n in range(2)]
        wbs = [keep.tile([P, BLK], U8, name=f"wbs{n}", align_bytes=64) for n in range(2)]

        def load_x(g):
            src = x_bytes[first[g] : first[g] + P * GROUPS[g], :].rearrange("(p a) k -> p a k", a=GROUPS[g])
            nc.sync.dma_start(out=xb[g][:], in_=src)

        nc.vector.memset(warm[:], 0.0)
        nc.vector.memset(wsr[:].bitcast(I32), 0)
        nc.scalar.activation(out=warm[:], in_=warm[:], func=ACT.Relu)
        make_identity(nc, ident[:])
        load_x(0)
        nc.sync.dma_start(out=sc[:], in_=x_scale.rearrange("o k -> (o k)").partition_broadcast(P))
        nc.sync.dma_start(out=w1r[:], in_=W1_words[0])
        for q in range(4):
            nc.sync.dma_start(
                out=wsr[32 * q : 32 * q + 4, :].bitcast(I32), in_=W1_scales[0, 4 * q : 4 * q + 4, :].bitcast(I32)
            )
        load_x(1)
        nc.sync.dma_start(out=b1c[:], in_=b1.rearrange("(n p t) -> p n t", n=2, t=4))
        nc.sync.dma_start(out=wbr[1][:], in_=Wb[1].rearrange("(p t) k -> p t k", t=4))
        nc.sync.dma_start(out=bbc[:], in_=bb[BLK:HID].rearrange("(p t) -> p t", t=4))
        nc.sync.dma_start(out=wbr[0][:], in_=Wb[0].rearrange("(t p) k -> p t k", p=P))
        nc.sync.dma_start(out=bbr[:], in_=bb[0:BLK].partition_broadcast(P))
        for g in range(2, L):
            load_x(g)

        xs, xg, xc, xsc = {}, {}, {}, {}
        xt, hp, hg, hc, hs = {}, {}, {}, {}, {}
        y1, y0, yt, tr, o = {}, {}, {}, {}, {}

        def width(g):
            return P * GROUPS[g]

        def halves(g):
            return GROUPS[g] // 2

        def scale_x(g, h):
            if h == 0:
                xs[g] = work.tile([P, GROUPS[g], IN], BF16, name="xs", tag="xs")
            if h >= halves(g):
                return
            for a in (2 * h, 2 * h + 1):
                nc.vector.tensor_tensor(out=xs[g][:, a, :], in0=xb[g][:, a, :].bitcast(FP8), in1=sc[:], op=ALU.mult)

        def turn(rows, a0, key):
            xt[key] = psum.tile([P, 2, 2 * P], F32, name="xt", tag="xt", bufs=2)
            for a in (0, 1):
                words = rows[:, a0 + a, :].bitcast(F32)
                for u in (0, 1):
                    nc.tensor.transpose(xt[key][:, u, a * P : (a + 1) * P], words[:, u : 2 * P : 2], ident[:])

        def turn_x(g, h):
            if h < halves(g):
                turn(xs[g], 2 * h, (g, h))

        def unload(dst, h, key):
            cols = dst[:, 2 * P * h : 2 * P * (h + 1), :].rearrange("p r t -> p (r t)").bitcast(F32)
            nc.scalar.copy(out=cols.rearrange("p (r u) -> p r u", u=2), in_=xt[key][:].rearrange("p u r -> p r u"))

        def unload_x(g, h):
            if h == 0:
                xg[g] = work.tile([P, width(g), 4], BF16, name="xg", tag="xg", align_bytes=64)
            if h < halves(g):
                unload(xg[g], h, (g, h))

        def quantize(src, codes, scales):
            nc.vector.quantize_mx(out=codes.bitcast(FP8X4), scales=scales, in_=src.rearrange("p r t -> p (r t)"))

        def quant_x(g):
            xc[g] = work.tile([P, width(g)], U32, name="xc", tag="xc", align_bytes=64)
            xsc[g] = work.tile([P, width(g)], U8, name="xsc", tag="xsc", align_bytes=64)
            quantize(xg[g][:], xc[g][:], xsc[g][:])

        def stage1(g, n, t):
            acc = psum.tile([P, width(g)], F32, name="h", tag="h", bufs=2)
            nc.tensor.matmul_mx(
                out=acc[:],
                lhsT=w1p[:, n, t].rearrange("p m b -> p (m b)").bitcast(FP4X4),
                lhsT_scale=wsp[:, n, t, :],
                rhs=xc[g][:].bitcast(FP8X4),
                rhs_scale=xsc[g][:],
                start=True,
                stop=True,
            )
            if t == 0:
                hp[g, n] = work.tile([P, 4, width(g)], BF16, name="hp", tag="hp", bufs=4)
            nc.scalar.activation(out=hp[g, n][:, t, :], in_=acc[:], func=ACT.Relu, bias=b1c[:, n, t : t + 1])

        def interleave(g, n):
            hg[g, n] = work.tile([P, width(g), 4], BF16, name="hg", tag="hg", align_bytes=64)
            nc.vector.tensor_copy(
                out=hg[g, n][:].rearrange("p (c i) t -> p c t i", i=4),
                in_=hp[g, n][:].rearrange("p t (c i) -> p c t i", i=4),
            )

        def quant_h(g, n):
            hc[g, n] = work.tile([P, width(g)], U32, name="hc", tag="hc", align_bytes=64, bufs=4)
            hs[g, n] = work.tile([P, width(g)], U8, name="hs", tag="hs", align_bytes=64, bufs=4)
            quantize(hg[g, n][:], hc[g, n][:], hs[g, n][:])

        def stage2_channels(g, t):
            y1[g, t] = psum.tile([P, width(g)], F32, name="y", tag="y", bufs=2)
            cols = slice(t * P, (t + 1) * P)
            nc.tensor.matmul_mx(
                out=y1[g, t][:],
                lhsT=wbc[1][:, cols].bitcast(FP8X4),
                lhsT_scale=wbs[1][:, cols],
                rhs=hc[g, 1][:].bitcast(FP8X4),
                rhs_scale=hs[g, 1][:],
                start=True,
                stop=True,
            )

        def relu_channels(g, t):
            yt[g, t] = work.tile([P, width(g)], F32, name="yt", tag="yt", bufs=8)
            nc.scalar.activation(out=yt[g, t][:], in_=y1[g, t][:], func=ACT.Relu, bias=bbc[:, t : t + 1])

        def turn_back(g, a):
            if a >= GROUPS[g]:
                return
            tr[g, a] = psum.tile([P, 4, P], F32, name="tr", tag="tr", bufs=2)
            for t in range(4):
                nc.tensor.transpose(tr[g, a][:, t, :], yt[g, t][:, a * P : (a + 1) * P], ident[:])

        def store_turned(g, a, on_vector):
            if a >= GROUPS[g]:
                return
            dst = o[g][:, a, BLK:HID].rearrange("p (r t) -> p r t", t=4)
            src = tr[g, a][:].rearrange("p t r -> p r t")
            if on_vector:
                nc.vector.tensor_copy(out=dst, in_=src)
            else:
                nc.scalar.copy(out=dst, in_=src)
            rows = out[first[g] : first[g] + width(g), :].rearrange("(p a) c -> p a c", a=GROUPS[g])
            nc.sync.dma_start(out=rows[:, a, :], in_=o[g][:, a, :])

        def stage2_tokens(g, a):
            if a >= GROUPS[g]:
                return
            y0[g, a] = psum.tile([P, BLK], F32, name="y", tag="y", bufs=2)
            cols = slice(a * P, (a + 1) * P)
            nc.tensor.matmul_mx(
                out=y0[g, a][:],
                lhsT=hc[g, 0][:, cols].bitcast(FP8X4),
                lhsT_scale=hs[g, 0][:, cols],
                rhs=wbc[0][:].bitcast(FP8X4),
                rhs_scale=wbs[0][:],
                start=True,
                stop=True,
            )

        def bias_tokens(g, a):
            if a >= GROUPS[g]:
                return
            if a == 0:
                o[g] = work.tile([P, GROUPS[g], HID], F32, name="o", tag="o")
            part = o[g][:, a, 0:BLK]
            nc.vector.tensor_tensor(out=part, in0=y0[g, a][:], in1=bbr[:], op=ALU.add)
            if a % 2 == 1:
                pair = o[g][:, a - 1 : a + 1, 0:BLK]
                nc.vector.tensor_scalar(out=pair, in0=pair, scalar1=0.0, scalar2=None, op0=ALU.max)

        def weights2(n):
            wg = work.tile([P, BLK, 4], BF16, name="wg", tag="wg", align_bytes=64, bufs=2)
            for h in (0, 1):
                turn(wbr[n], 2 * h, ("w", n, h))
                unload(wg, h, ("w", n, h))
            quantize(wg[:], wbc[n][:], wbs[n][:])

        def permute_w1(n):
            nc.vector.tensor_copy(
                out=w1p[:, n], in_=w1r[:].rearrange("p (n m t b) -> p n t m b", n=2, t=4, b=2)[:, n]
            )
            nc.gpsimd.tensor_copy(out=wsp[:, n], in_=wsr[:].rearrange("p (n m t) -> p n t m", n=2, t=4)[:, n])

        def slot(g):
            now, prev, nxt, far = 0 <= g < L, 0 <= g - 1 < L, 0 <= g + 1 < L, 0 <= g + 2 < L
            if prev:
                bias_tokens(g - 1, 0)
            if now:
                stage1(g, 1, 0)
                stage1(g, 1, 1)
            if prev:
                stage2_tokens(g - 1, 2)
                bias_tokens(g - 1, 1)
            if now:
                stage1(g, 1, 2)
            if prev:
                stage2_tokens(g - 1, 3)
            if now:
                stage1(g, 1, 3)
            if prev:
                bias_tokens(g - 1, 2)
                bias_tokens(g - 1, 3)
                turn_back(g - 1, 0)
                turn_back(g - 1, 1)
            if now:
                interleave(g, 1)
                for t in range(4):
                    stage1(g, 0, t)
            if prev:
                store_turned(g - 1, 0, False)
                store_turned(g - 1, 1, GROUPS[g - 1] == 2)
            if far:
                scale_x(g + 2, 0)
            if g == -2:
                permute_w1(1)
                permute_w1(0)
            if now:
                quant_h(g, 1)
                stage2_channels(g, 0)
                stage2_channels(g, 1)
                interleave(g, 0)
            if prev:
                turn_back(g - 1, 2)
                turn_back(g - 1, 3)
                store_turned(g - 1, 2, False)
            if nxt:
                unload_x(g + 1, 0)
                unload_x(g + 1, 1)
            if g == -1:
                quant_x(0)
                weights2(1)
            if g == 0:
                weights2(0)
            if far:
                turn_x(g + 2, 0)
                scale_x(g + 2, 1)
                turn_x(g + 2, 1)
            if now:
                relu_channels(g, 0)
                stage2_channels(g, 2)
                relu_channels(g, 1)
                stage2_channels(g, 3)
                relu_channels(g, 2)
                relu_channels(g, 3)
                quant_h(g, 0)
            if prev:
                store_turned(g - 1, 3, False)
            if nxt and g >= 0:
                quant_x(g + 1)
            if now:
                stage2_tokens(g, 0)
                stage2_tokens(g, 1)

        for g in range(-2, L + 1):
            slot(g)
